import numpy as np
import ml_dtypes


def mxq(x, axis, fmt="e4m3"):
    dtype, down = {"e4m3": (ml_dtypes.float8_e4m3fn, 7), "e5m2": (ml_dtypes.float8_e5m2, 14)}[fmt]
    v = np.moveaxis(np.asarray(x, np.float32).astype(ml_dtypes.bfloat16).astype(np.float64), axis, -1)
    blocks = v.reshape(v.shape[:-1] + (-1, 32))
    amax = np.abs(blocks).max(-1, keepdims=True)
    byte = np.maximum(np.where(amax > 0, np.frexp(amax)[1] - 1 + 127, 0) - down, 1)
    scale = np.exp2(byte - 127.0)
    codes = (blocks / scale).astype(np.float32).astype(dtype).astype(np.float64)
    return np.moveaxis((codes * scale).reshape(v.shape), -1, axis)


WIDE = False


def mx_kscale(k):
    if not WIDE:
        return np.ones(k)
    levels = np.array([10, -10, 5, -5, 0])
    a = np.random.permutation(np.resize(levels, k // 512 * 4)).reshape(k // 512, 4)
    idx = np.arange(k)
    return np.exp2(a[idx // 512, idx % 128 // 32])


BF16 = ml_dtypes.bfloat16


def bf(x):
    return np.asarray(x, np.float32).astype(BF16)


def f64(x):
    return np.asarray(x).astype(np.float64)


B, S, D, M, R = 128, 4, 512, 8, 512
LN_EPS = 1e-5


def sigmoid(v):
    return 1.0 / (1.0 + np.exp(-v))


def layer_norm(x):
    mu = np.mean(x, axis=-1, keepdims=True)
    var = np.var(x, axis=-1, keepdims=True)
    return (x - mu) / np.sqrt(var + LN_EPS)


def setup_inputs():
    s, t = mx_kscale(D), mx_kscale(R)
    return {"interface": bf(np.random.standard_normal((B, S, D)) * np.sqrt(S) * s),
            "memory": bf(0.5 + np.random.standard_normal((B, M, D))),
            "W_write_key": bf(np.random.standard_normal((R, D)) / np.sqrt(D) / s[None, :] * t[:, None]),
            "W_write_erase": bf(np.random.standard_normal((D, R)) * 1.5 / np.sqrt(R) / t[None, :]),
            "W_write_add": bf(np.random.standard_normal((D, R)) / np.sqrt(R) / t[None, :])}


def reference(interface, memory, W_write_key, W_write_erase, W_write_add):
    i_mean = np.mean(f64(interface), axis=1)
    i_proj = mxq(i_mean, 1, "e4m3") @ mxq(f64(W_write_key), 1, "e4m3").T
    pq = mxq(i_proj, 1, "e4m3")
    erase = sigmoid(pq @ mxq(f64(W_write_erase), 1, "e4m3").T)[:, None, :]
    add = (pq @ mxq(f64(W_write_add), 1, "e4m3").T)[:, None, :]
    return layer_norm(f64(memory) * (1.0 - erase) + add)

@@ -1,0 +1,201 @@
+from contextlib import ExitStack
+
+import concourse.mybir as mybir
+from concourse.masks import make_identity
+
+F32 = mybir.dt.float32
+BF16 = mybir.dt.bfloat16
+U32 = mybir.dt.uint32
+U8 = mybir.dt.uint8
+FP8X4 = mybir.dt.float8_e4m3fn_x4
+ALU = mybir.AluOpType
+ACT = mybir.ActivationFunctionType
+
+P = 128
+POSITIONS = 4
+SLOTS = 8
+D = 512
+PACK = 4
+CHUNKS = D // P
+WORDS = D // 2
+LN_EPS = 1e-5
+VECTOR_NORM_SLOTS = 2
+
+FLOPS = 3 * 2 * P * D * D
+
+
+def transpose_and_quantise(nc, banks, pool, weight_sb, identity, copy_out, name):
+    words = weight_sb[:].bitcast(F32)
+    grouped = pool.tile([P, D * PACK], BF16, align_bytes=64, name=name + "_grouped")
+    grouped_words = grouped[:].bitcast(F32)
+    for half in range(2):
+        bank = banks.tile([P, 2, 2 * P], F32, tag="bank", name=name + "_bank")
+        for u in range(2):
+            for j in range(2):
+                c = 2 * half + j
+                first = WORDS * c + P * u
+                nc.tensor.transpose(bank[:, u, P * j : P * (j + 1)], words[:, first : first + P], identity[:])
+        copy_out(
+            out=grouped_words[:, D * half : D * (half + 1)].rearrange("p (n u) -> p n u", u=2),
+            in_=bank[:].rearrange("p u n -> p n u"),
+        )
+    codes = pool.tile([P, D], U32, align_bytes=64, name=name + "_codes")
+    scales = pool.tile([P, D], U8, align_bytes=64, name=name + "_scales")
+    nc.vector.quantize_mx(out=codes[:].bitcast(FP8X4), scales=scales[:], in_=grouped[:])
+    return codes, scales
+
+
+def quantise_activation(nc, pool, grouped, name):
+    codes = pool.tile([P, P], U32, align_bytes=64, name=name + "_codes")
+    scales = pool.tile([P, P], U8, align_bytes=64, name=name + "_scales")
+    nc.vector.quantize_mx(out=codes[:].bitcast(FP8X4), scales=scales[:], in_=grouped[:])
+    return codes, scales
+
+
+def tile_ultralightweightmemory_pa_s_kernel(
+    tc, interface, memory, W_write_key, W_write_erase, W_write_add, out
+):
+    nc = tc.nc
+    with ExitStack() as stack:
+        pool = stack.enter_context(tc.tile_pool(name="resident", bufs=1))
+        banks = stack.enter_context(tc.psum_pool(name="banks", bufs=4))
+        sums = stack.enter_context(tc.psum_pool(name="sums", bufs=1))
+
+        iface_sb = pool.tile([P, POSITIONS, D], BF16)
+        nc.sync.dma_start(out=iface_sb[:], in_=interface)
+        key_sb = pool.tile([P, CHUNKS * D], BF16)
+        key_rows = W_write_key.rearrange("(u q e) k -> u q (e k)", u=2, e=2)
+        for u in range(2):
+            nc.sync.dma_start(out=key_sb[:, 2 * D * u : 2 * D * (u + 1)], in_=key_rows[u])
+        erase_sb = pool.tile([P, CHUNKS * D], BF16)
+        nc.sync.dma_start(
+            out=erase_sb[:].rearrange("q (c k) -> q c k", c=CHUNKS),
+            in_=W_write_erase.rearrange("(c q) k -> q c k", q=P),
+        )
+        add_sb = pool.tile([P, CHUNKS * D], BF16)
+        nc.sync.dma_start(
+            out=add_sb[:].rearrange("q (c k) -> q c k", c=CHUNKS),
+            in_=W_write_add.rearrange("(c q) k -> q c k", q=P),
+        )
+        memory_sb = pool.tile([P, SLOTS, D], BF16)
+        nc.sync.dma_start(out=memory_sb[:], in_=memory)
+
+        identity = pool.tile([P, P], F32)
+        make_identity(nc, identity[:])
+        eps_col = pool.tile([P, 1], F32)
+        nc.vector.memset(eps_col[:], LN_EPS)
+        warm_col = pool.tile([P, 2], F32)
+        nc.scalar.activation(out=warm_col[:, 0:1], in_=eps_col[:], func=ACT.Sigmoid)
+
+        pair_sums = pool.tile([P, 2, D], F32)
+        nc.vector.tensor_tensor(out=pair_sums[:], in0=iface_sb[:, 0:2, :], in1=iface_sb[:, 2:4, :], op=ALU.add)
+        position_sum = pool.tile([P, D], F32)
+        nc.vector.tensor_tensor(
+            out=position_sum[:].rearrange("b (u e q) -> b u e q", u=2, e=2),
+            in0=pair_sums[:, 0, :].rearrange("b (u q e) -> b u e q", u=2, e=2),
+            in1=pair_sums[:, 1, :].rearrange("b (u q e) -> b u e q", u=2, e=2),
+            op=ALU.add,
+        )
+
+        key_codes, key_scales = transpose_and_quantise(nc, banks, pool, key_sb, identity, nc.scalar.copy, "key")
+
+        sum_T = sums.tile([P, PACK, P], F32)
+        for t in range(PACK):
+            nc.tensor.transpose(sum_T[:, t, :], position_sum[:, P * t : P * (t + 1)], identity[:])
+        mean_grouped = pool.tile([P, P * PACK], BF16, align_bytes=64)
+        nc.scalar.mul(
+            out=mean_grouped[:].rearrange("p (b t) -> p b t", t=PACK),
+            in_=sum_T[:].rearrange("p t b -> p b t"),
+            mul=1.0 / POSITIONS,
+        )
+        mean_codes, mean_scales = quantise_activation(nc, pool, mean_grouped, "mean")
+
+        proj_T = sums.tile([P, PACK, P], F32)
+        for t in range(PACK):
+            nc.tensor.matmul_mx(
+                out=proj_T[:, t, :],
+                lhsT=key_codes[:, P * t : P * (t + 1)].bitcast(FP8X4),
+                lhsT_scale=key_scales[:, P * t : P * (t + 1)],
+                rhs=mean_codes[:].bitcast(FP8X4),
+                rhs_scale=mean_scales[:],
+                start=True,
+                stop=True,
+            )
+        proj_grouped = pool.tile([P, P * PACK], BF16, align_bytes=64)
+        nc.scalar.copy(
+            out=proj_grouped[:].rearrange("p (b t) -> p b t", t=PACK),
+            in_=proj_T[:].rearrange("p t b -> p b t"),
+        )
+        erase_codes, erase_scales = transpose_and_quantise(
+            nc, banks, pool, erase_sb, identity, nc.vector.tensor_copy, "erase"
+        )
+        proj_codes, proj_scales = quantise_activation(nc, pool, proj_grouped, "proj")
+        add_codes, add_scales = transpose_and_quantise(nc, banks, pool, add_sb, identity, nc.scalar.copy, "add")
+
+        erase_ps = sums.tile([P, D], F32)
+        nc.tensor.matmul_mx(
+            out=erase_ps[:],
+            lhsT=proj_codes[:].bitcast(FP8X4),
+            lhsT_scale=proj_scales[:],
+            rhs=erase_codes[:].bitcast(FP8X4),
+            rhs_scale=erase_scales[:],
+            start=True,
+            stop=True,
+        )
+        add_ps = sums.tile([P, D], F32)
+        nc.tensor.matmul_mx(
+            out=add_ps[:],
+            lhsT=proj_codes[:].bitcast(FP8X4),
+            lhsT_scale=proj_scales[:],
+            rhs=add_codes[:].bitcast(FP8X4),
+            rhs_scale=add_scales[:],
+            start=True,
+            stop=True,
+        )
+        keep = pool.tile([P, D], F32)
+        nc.scalar.activation(out=keep[:], in_=erase_ps[:], func=ACT.Sigmoid, scale=-1.0)
+        nc.scalar.activation(out=warm_col[:, 1:2], in_=keep[:, 0:1], func=ACT.Abs_reciprocal_sqrt)
+
+        gated = pool.tile([P, SLOTS, D], F32)
+        x = pool.tile([P, SLOTS, D], F32)
+        squares = pool.tile([P, SLOTS, D], F32)
+        normed = pool.tile([P, SLOTS, D], F32)
+        x_sum = pool.tile([P, SLOTS], F32)
+        neg_mean = pool.tile([P, SLOTS], F32)
+        sq_sum = pool.tile([P, SLOTS], F32)
+        rstd = pool.tile([P, SLOTS], F32)
+        shift = pool.tile([P, SLOTS], F32)
+        for m in range(SLOTS):
+            col = slice(m, m + 1)
+            nc.vector.tensor_tensor(out=gated[:, m, :], in0=memory_sb[:, m, :], in1=keep[:], op=ALU.mult)
+            nc.vector.scalar_tensor_tensor(
+                out=x[:, m, :],
+                in0=gated[:, m, :],
+                scalar=1.0,
+                in1=add_ps[:],
+                op0=ALU.mult,
+                op1=ALU.add,
+                accum_out=x_sum[:, col],
+            )
+            nc.vector.tensor_scalar_mul(out=neg_mean[:, col], in0=x_sum[:, col], scalar1=-1.0 / D)
+            nc.scalar.activation(
+                out=squares[:, m, :], in_=x[:, m, :], func=ACT.Square, bias=neg_mean[:, col], accum_out=sq_sum[:, col]
+            )
+            nc.scalar.activation(
+                out=rstd[:, col], in_=sq_sum[:, col], func=ACT.Abs_reciprocal_sqrt, scale=1.0 / D, bias=eps_col[:]
+            )
+            if m < SLOTS - VECTOR_NORM_SLOTS:
+                nc.scalar.mul(out=shift[:, col], in_=neg_mean[:, col], mul=rstd[:, col])
+                nc.scalar.activation(
+                    out=normed[:, m, :], in_=x[:, m, :], func=ACT.Identity, scale=rstd[:, col], bias=shift[:, col]
+                )
+            else:
+                nc.vector.tensor_scalar(
+                    out=normed[:, m, :],
+                    in0=x[:, m, :],
+                    scalar1=neg_mean[:, col],
+                    scalar2=rstd[:, col],
+                    op0=ALU.add,
+                    op1=ALU.mult,
+                )
+            nc.sync.dma_start(out=out[:, m, :], in_=normed[:, m, :])

@@ -24,7 +24,7 @@ VECTOR_NORM_SLOTS = 2
 FLOPS = 3 * 2 * P * D * D
 
 
-def transpose_and_quantise(nc, banks, pool, weight_sb, identity, copy_out, name):
+def transpose_words(nc, banks, pool, weight_sb, identity, copy_out, name):
     words = weight_sb[:].bitcast(F32)
     grouped = pool.tile([P, D * PACK], BF16, align_bytes=64, name=name + "_grouped")
     grouped_words = grouped[:].bitcast(F32)
@@ -39,17 +39,26 @@ def transpose_and_quantise(nc, banks, pool, weight_sb, identity, copy_out, name)
             out=grouped_words[:, D * half : D * (half + 1)].rearrange("p (n u) -> p n u", u=2),
             in_=bank[:].rearrange("p u n -> p n u"),
         )
-    codes = pool.tile([P, D], U32, align_bytes=64, name=name + "_codes")
-    scales = pool.tile([P, D], U8, align_bytes=64, name=name + "_scales")
+    return grouped
+
+
+def quantise(nc, pool, grouped, columns, name):
+    codes = pool.tile([P, columns], U32, align_bytes=64, name=name + "_codes")
+    scales = pool.tile([P, columns], U8, align_bytes=64, name=name + "_scales")
     nc.vector.quantize_mx(out=codes[:].bitcast(FP8X4), scales=scales[:], in_=grouped[:])
     return codes, scales
 
 
-def quantise_activation(nc, pool, grouped, name):
-    codes = pool.tile([P, P], U32, align_bytes=64, name=name + "_codes")
-    scales = pool.tile([P, P], U8, align_bytes=64, name=name + "_scales")
-    nc.vector.quantize_mx(out=codes[:].bitcast(FP8X4), scales=scales[:], in_=grouped[:])
-    return codes, scales
+def one_pass(nc, acc, stationary, moving):
+    nc.tensor.matmul_mx(
+        out=acc,
+        lhsT=stationary[0].bitcast(FP8X4),
+        lhsT_scale=stationary[1],
+        rhs=moving[0].bitcast(FP8X4),
+        rhs_scale=moving[1],
+        start=True,
+        stop=True,
+    )
 
 
 def tile_ultralightweightmemory_pa_s_kernel(
@@ -60,6 +69,7 @@ def tile_ultralightweightmemory_pa_s_kernel(
         pool = stack.enter_context(tc.tile_pool(name="resident", bufs=1))
         banks = stack.enter_context(tc.psum_pool(name="banks", bufs=4))
         sums = stack.enter_context(tc.psum_pool(name="sums", bufs=1))
+        stack.enter_context(tc.manual_schedule())
 
         iface_sb = pool.tile([P, POSITIONS, D], BF16)
         nc.sync.dma_start(out=iface_sb[:], in_=interface)
@@ -97,8 +107,7 @@ def tile_ultralightweightmemory_pa_s_kernel(
             op=ALU.add,
         )
 
-        key_codes, key_scales = transpose_and_quantise(nc, banks, pool, key_sb, identity, nc.scalar.copy, "key")
-
+        key_grouped = transpose_words(nc, banks, pool, key_sb, identity, nc.scalar.copy, "key")
         sum_T = sums.tile([P, PACK, P], F32)
         for t in range(PACK):
             nc.tensor.transpose(sum_T[:, t, :], position_sum[:, P * t : P * (t + 1)], identity[:])
@@ -108,53 +117,33 @@ def tile_ultralightweightmemory_pa_s_kernel(
             in_=sum_T[:].rearrange("p t b -> p b t"),
             mul=1.0 / POSITIONS,
         )
-        mean_codes, mean_scales = quantise_activation(nc, pool, mean_grouped, "mean")
+        key_codes, key_scales = quantise(nc, pool, key_grouped, D, "key")
+        mean_codes, mean_scales = quantise(nc, pool, mean_grouped, P, "mean")
+
+        erase_grouped = transpose_words(nc, banks, pool, erase_sb, identity, nc.scalar.copy, "erase")
 
         proj_T = sums.tile([P, PACK, P], F32)
         for t in range(PACK):
-            nc.tensor.matmul_mx(
-                out=proj_T[:, t, :],
-                lhsT=key_codes[:, P * t : P * (t + 1)].bitcast(FP8X4),
-                lhsT_scale=key_scales[:, P * t : P * (t + 1)],
-                rhs=mean_codes[:].bitcast(FP8X4),
-                rhs_scale=mean_scales[:],
-                start=True,
-                stop=True,
-            )
+            rows = slice(P * t, P * (t + 1))
+            one_pass(nc, proj_T[:, t, :], (key_codes[:, rows], key_scales[:, rows]), (mean_codes[:], mean_scales[:]))
         proj_grouped = pool.tile([P, P * PACK], BF16, align_bytes=64)
         nc.scalar.copy(
             out=proj_grouped[:].rearrange("p (b t) -> p b t", t=PACK),
             in_=proj_T[:].rearrange("p t b -> p b t"),
         )
-        erase_codes, erase_scales = transpose_and_quantise(
-            nc, banks, pool, erase_sb, identity, nc.vector.tensor_copy, "erase"
-        )
-        proj_codes, proj_scales = quantise_activation(nc, pool, proj_grouped, "proj")
-        add_codes, add_scales = transpose_and_quantise(nc, banks, pool, add_sb, identity, nc.scalar.copy, "add")
+        erase_codes, erase_scales = quantise(nc, pool, erase_grouped, D, "erase")
+        proj_codes, proj_scales = quantise(nc, pool, proj_grouped, P, "proj")
+
+        add_grouped = transpose_words(nc, banks, pool, add_sb, identity, nc.scalar.copy, "add")
 
         erase_ps = sums.tile([P, D], F32)
-        nc.tensor.matmul_mx(
-            out=erase_ps[:],
-            lhsT=proj_codes[:].bitcast(FP8X4),
-            lhsT_scale=proj_scales[:],
-            rhs=erase_codes[:].bitcast(FP8X4),
-            rhs_scale=erase_scales[:],
-            start=True,
-            stop=True,
-        )
-        add_ps = sums.tile([P, D], F32)
-        nc.tensor.matmul_mx(
-            out=add_ps[:],
-            lhsT=proj_codes[:].bitcast(FP8X4),
-            lhsT_scale=proj_scales[:],
-            rhs=add_codes[:].bitcast(FP8X4),
-            rhs_scale=add_scales[:],
-            start=True,
-            stop=True,
-        )
+        one_pass(nc, erase_ps[:], (proj_codes[:], proj_scales[:]), (erase_codes[:], erase_scales[:]))
         keep = pool.tile([P, D], F32)
         nc.scalar.activation(out=keep[:], in_=erase_ps[:], func=ACT.Sigmoid, scale=-1.0)
         nc.scalar.activation(out=warm_col[:, 1:2], in_=keep[:, 0:1], func=ACT.Abs_reciprocal_sqrt)
+        add_codes, add_scales = quantise(nc, pool, add_grouped, D, "add")
+        add_ps = sums.tile([P, D], F32)
+        one_pass(nc, add_ps[:], (proj_codes[:], proj_scales[:]), (add_codes[:], add_scales[:]))
 
         gated = pool.tile([P, SLOTS, D], F32)
         x = pool.tile([P, SLOTS, D], F32)
@@ -165,9 +154,11 @@ def tile_ultralightweightmemory_pa_s_kernel(
         sq_sum = pool.tile([P, SLOTS], F32)
         rstd = pool.tile([P, SLOTS], F32)
         shift = pool.tile([P, SLOTS], F32)
-        for m in range(SLOTS):
-            col = slice(m, m + 1)
+
+        def gate(m):
             nc.vector.tensor_tensor(out=gated[:, m, :], in0=memory_sb[:, m, :], in1=keep[:], op=ALU.mult)
+
+        def add_and_sum(m):
             nc.vector.scalar_tensor_tensor(
                 out=x[:, m, :],
                 in0=gated[:, m, :],
@@ -175,17 +166,31 @@ def tile_ultralightweightmemory_pa_s_kernel(
                 in1=add_ps[:],
                 op0=ALU.mult,
                 op1=ALU.add,
-                accum_out=x_sum[:, col],
+                accum_out=x_sum[:, m : m + 1],
             )
-            nc.vector.tensor_scalar_mul(out=neg_mean[:, col], in0=x_sum[:, col], scalar1=-1.0 / D)
+            nc.gpsimd.tensor_scalar_mul(out=neg_mean[:, m : m + 1], in0=x_sum[:, m : m + 1], scalar1=-1.0 / D)
+
+        def spread(m):
             nc.scalar.activation(
-                out=squares[:, m, :], in_=x[:, m, :], func=ACT.Square, bias=neg_mean[:, col], accum_out=sq_sum[:, col]
+                out=squares[:, m, :],
+                in_=x[:, m, :],
+                func=ACT.Square,
+                scale=-1.0 * D,
+                bias=x_sum[:, m : m + 1],
+                accum_out=sq_sum[:, m : m + 1],
             )
             nc.scalar.activation(
-                out=rstd[:, col], in_=sq_sum[:, col], func=ACT.Abs_reciprocal_sqrt, scale=1.0 / D, bias=eps_col[:]
+                out=rstd[:, m : m + 1],
+                in_=sq_sum[:, m : m + 1],
+                func=ACT.Abs_reciprocal_sqrt,
+                scale=1.0 / (D * D * D),
+                bias=eps_col[:],
             )
+
+        def normalise_and_store(m):
+            col = slice(m, m + 1)
             if m < SLOTS - VECTOR_NORM_SLOTS:
-                nc.scalar.mul(out=shift[:, col], in_=neg_mean[:, col], mul=rstd[:, col])
+                nc.gpsimd.tensor_tensor(out=shift[:, col], in0=neg_mean[:, col], in1=rstd[:, col], op=ALU.mult)
                 nc.scalar.activation(
                     out=normed[:, m, :], in_=x[:, m, :], func=ACT.Identity, scale=rstd[:, col], bias=shift[:, col]
                 )
@@ -199,3 +204,13 @@ def tile_ultralightweightmemory_pa_s_kernel(
                     op1=ALU.mult,
                 )
             nc.sync.dma_start(out=out[:, m, :], in_=normed[:, m, :])
+
+        gate(0)
+        for m in range(SLOTS):
+            if m + 1 < SLOTS:
+                gate(m + 1)
+            add_and_sum(m)
+            spread(m)
+            if m > 0:
+                normalise_and_store(m - 1)
+        normalise_and_store(SLOTS - 1)

@@ -19,7 +19,8 @@ PACK = 4
 CHUNKS = D // P
 WORDS = D // 2
 LN_EPS = 1e-5
-VECTOR_NORM_SLOTS = 2
+VECTOR_NORM_SLOTS = 3
+LAG = 2
 
 FLOPS = 3 * 2 * P * D * D
 
@@ -170,7 +171,7 @@ def tile_ultralightweightmemory_pa_s_kernel(
             )
             nc.gpsimd.tensor_scalar_mul(out=neg_mean[:, m : m + 1], in0=x_sum[:, m : m + 1], scalar1=-1.0 / D)
 
-        def spread(m):
+        def square_and_sum(m):
             nc.scalar.activation(
                 out=squares[:, m, :],
                 in_=x[:, m, :],
@@ -179,6 +180,8 @@ def tile_ultralightweightmemory_pa_s_kernel(
                 bias=x_sum[:, m : m + 1],
                 accum_out=sq_sum[:, m : m + 1],
             )
+
+        def scale_and_shift(m):
             nc.scalar.activation(
                 out=rstd[:, m : m + 1],
                 in_=sq_sum[:, m : m + 1],
@@ -186,11 +189,14 @@ def tile_ultralightweightmemory_pa_s_kernel(
                 scale=1.0 / (D * D * D),
                 bias=eps_col[:],
             )
+            if m < SLOTS - VECTOR_NORM_SLOTS:
+                nc.gpsimd.tensor_tensor(
+                    out=shift[:, m : m + 1], in0=neg_mean[:, m : m + 1], in1=rstd[:, m : m + 1], op=ALU.mult
+                )
 
         def normalise_and_store(m):
             col = slice(m, m + 1)
             if m < SLOTS - VECTOR_NORM_SLOTS:
-                nc.gpsimd.tensor_tensor(out=shift[:, col], in0=neg_mean[:, col], in1=rstd[:, col], op=ALU.mult)
                 nc.scalar.activation(
                     out=normed[:, m, :], in_=x[:, m, :], func=ACT.Identity, scale=rstd[:, col], bias=shift[:, col]
                 )
@@ -206,11 +212,13 @@ def tile_ultralightweightmemory_pa_s_kernel(
             nc.sync.dma_start(out=out[:, m, :], in_=normed[:, m, :])
 
         gate(0)
-        for m in range(SLOTS):
+        for m in range(SLOTS + LAG):
             if m + 1 < SLOTS:
                 gate(m + 1)
-            add_and_sum(m)
-            spread(m)
-            if m > 0:
-                normalise_and_store(m - 1)
-        normalise_and_store(SLOTS - 1)
+            if m < SLOTS:
+                add_and_sum(m)
+                square_and_sum(m)
+            if m >= LAG:
+                normalise_and_store(m - LAG)
+            if m < SLOTS:
+                scale_and_shift(m)

@@ -20,6 +20,8 @@ CHUNKS = D // P
 WORDS = D // 2
 LN_EPS = 1e-5
 VECTOR_NORM_SLOTS = 3
+GPSIMD_COLUMNS = 192
+VECTOR_COLUMNS = D - GPSIMD_COLUMNS
 LAG = 2
 
 FLOPS = 3 * 2 * P * D * D
@@ -156,8 +158,13 @@ def tile_ultralightweightmemory_pa_s_kernel(
         rstd = pool.tile([P, SLOTS], F32)
         shift = pool.tile([P, SLOTS], F32)
 
-        def gate(m):
-            nc.vector.tensor_tensor(out=gated[:, m, :], in0=memory_sb[:, m, :], in1=keep[:], op=ALU.mult)
+        def gate_on_vector(m):
+            cols = slice(0, D if m == 0 else VECTOR_COLUMNS)
+            nc.vector.tensor_tensor(out=gated[:, m, cols], in0=memory_sb[:, m, cols], in1=keep[:, cols], op=ALU.mult)
+
+        def gate_on_gpsimd(m):
+            cols = slice(VECTOR_COLUMNS, D)
+            nc.gpsimd.tensor_tensor(out=gated[:, m, cols], in0=memory_sb[:, m, cols], in1=keep[:, cols], op=ALU.mult)
 
         def add_and_sum(m):
             nc.vector.scalar_tensor_tensor(
@@ -169,7 +176,8 @@ def tile_ultralightweightmemory_pa_s_kernel(
                 op1=ALU.add,
                 accum_out=x_sum[:, m : m + 1],
             )
-            nc.gpsimd.tensor_scalar_mul(out=neg_mean[:, m : m + 1], in0=x_sum[:, m : m + 1], scalar1=-1.0 / D)
+            if m >= SLOTS - VECTOR_NORM_SLOTS:
+                nc.gpsimd.tensor_scalar_mul(out=neg_mean[:, m : m + 1], in0=x_sum[:, m : m + 1], scalar1=-1.0 / D)
 
         def square_and_sum(m):
             nc.scalar.activation(
@@ -190,8 +198,13 @@ def tile_ultralightweightmemory_pa_s_kernel(
                 bias=eps_col[:],
             )
             if m < SLOTS - VECTOR_NORM_SLOTS:
-                nc.gpsimd.tensor_tensor(
-                    out=shift[:, m : m + 1], in0=neg_mean[:, m : m + 1], in1=rstd[:, m : m + 1], op=ALU.mult
+                nc.gpsimd.tensor_scalar(
+                    out=shift[:, m : m + 1],
+                    in0=x_sum[:, m : m + 1],
+                    scalar1=rstd[:, m : m + 1],
+                    scalar2=-1.0 / D,
+                    op0=ALU.mult,
+                    op1=ALU.mult,
                 )
 
         def normalise_and_store(m):
@@ -211,10 +224,13 @@ def tile_ultralightweightmemory_pa_s_kernel(
                 )
             nc.sync.dma_start(out=out[:, m, :], in_=normed[:, m, :])
 
-        gate(0)
+        gate_on_vector(0)
+        gate_on_gpsimd(1)
         for m in range(SLOTS + LAG):
             if m + 1 < SLOTS:
-                gate(m + 1)
+                gate_on_vector(m + 1)
+            if m + 2 < SLOTS:
+                gate_on_gpsimd(m + 2)
             if m < SLOTS:
                 add_and_sum(m)
                 square_and_sum(m)

@@ -19,8 +19,8 @@ PACK = 4
 CHUNKS = D // P
 WORDS = D // 2
 LN_EPS = 1e-5
-VECTOR_NORM_SLOTS = 3
-GPSIMD_COLUMNS = 192
+VECTOR_NORM_SLOTS = 4
+GPSIMD_COLUMNS = 256
 VECTOR_COLUMNS = D - GPSIMD_COLUMNS
 LAG = 2
 

from contextlib import ExitStack

import concourse.mybir as mybir
from concourse.masks import make_identity

F32 = mybir.dt.float32
BF16 = mybir.dt.bfloat16
U32 = mybir.dt.uint32
U8 = mybir.dt.uint8
FP8X4 = mybir.dt.float8_e4m3fn_x4
ALU = mybir.AluOpType
ACT = mybir.ActivationFunctionType

P = 128
POSITIONS = 4
SLOTS = 8
D = 512
PACK = 4
CHUNKS = D // P
WORDS = D // 2
LN_EPS = 1e-5
VECTOR_NORM_SLOTS = 4
GPSIMD_COLUMNS = 256
VECTOR_COLUMNS = D - GPSIMD_COLUMNS
LAG = 2

FLOPS = 3 * 2 * P * D * D


def transpose_words(nc, banks, pool, weight_sb, identity, copy_out, name):
    words = weight_sb[:].bitcast(F32)
    grouped = pool.tile([P, D * PACK], BF16, align_bytes=64, name=name + "_grouped")
    grouped_words = grouped[:].bitcast(F32)
    for half in range(2):
        bank = banks.tile([P, 2, 2 * P], F32, tag="bank", name=name + "_bank")
        for u in range(2):
            for j in range(2):
                c = 2 * half + j
                first = WORDS * c + P * u
                nc.tensor.transpose(bank[:, u, P * j : P * (j + 1)], words[:, first : first + P], identity[:])
        copy_out(
            out=grouped_words[:, D * half : D * (half + 1)].rearrange("p (n u) -> p n u", u=2),
            in_=bank[:].rearrange("p u n -> p n u"),
        )
    return grouped


def quantise(nc, pool, grouped, columns, name):
    codes = pool.tile([P, columns], U32, align_bytes=64, name=name + "_codes")
    scales = pool.tile([P, columns], U8, align_bytes=64, name=name + "_scales")
    nc.vector.quantize_mx(out=codes[:].bitcast(FP8X4), scales=scales[:], in_=grouped[:])
    return codes, scales


def one_pass(nc, acc, stationary, moving):
    nc.tensor.matmul_mx(
        out=acc,
        lhsT=stationary[0].bitcast(FP8X4),
        lhsT_scale=stationary[1],
        rhs=moving[0].bitcast(FP8X4),
        rhs_scale=moving[1],
        start=True,
        stop=True,
    )


def tile_ultralightweightmemory_pa_s_kernel(
    tc, interface, memory, W_write_key, W_write_erase, W_write_add, out
):
    nc = tc.nc
    with ExitStack() as stack:
        pool = stack.enter_context(tc.tile_pool(name="resident", bufs=1))
        banks = stack.enter_context(tc.psum_pool(name="banks", bufs=4))
        sums = stack.enter_context(tc.psum_pool(name="sums", bufs=1))
        stack.enter_context(tc.manual_schedule())

        iface_sb = pool.tile([P, POSITIONS, D], BF16)
        nc.sync.dma_start(out=iface_sb[:], in_=interface)
        key_sb = pool.tile([P, CHUNKS * D], BF16)
        key_rows = W_write_key.rearrange("(u q e) k -> u q (e k)", u=2, e=2)
        for u in range(2):
            nc.sync.dma_start(out=key_sb[:, 2 * D * u : 2 * D * (u + 1)], in_=key_rows[u])
        erase_sb = pool.tile([P, CHUNKS * D], BF16)
        nc.sync.dma_start(
            out=erase_sb[:].rearrange("q (c k) -> q c k", c=CHUNKS),
            in_=W_write_erase.rearrange("(c q) k -> q c k", q=P),
        )
        add_sb = pool.tile([P, CHUNKS * D], BF16)
        nc.sync.dma_start(
            out=add_sb[:].rearrange("q (c k) -> q c k", c=CHUNKS),
            in_=W_write_add.rearrange("(c q) k -> q c k", q=P),
        )
        memory_sb = pool.tile([P, SLOTS, D], BF16)
        nc.sync.dma_start(out=memory_sb[:], in_=memory)

        identity = pool.tile([P, P], F32)
        make_identity(nc, identity[:])
        eps_col = pool.tile([P, 1], F32)
        nc.vector.memset(eps_col[:], LN_EPS)
        warm_col = pool.tile([P, 2], F32)
        nc.scalar.activation(out=warm_col[:, 0:1], in_=eps_col[:], func=ACT.Sigmoid)

        pair_sums = pool.tile([P, 2, D], F32)
        nc.vector.tensor_tensor(out=pair_sums[:], in0=iface_sb[:, 0:2, :], in1=iface_sb[:, 2:4, :], op=ALU.add)
        position_sum = pool.tile([P, D], F32)
        nc.vector.tensor_tensor(
            out=position_sum[:].rearrange("b (u e q) -> b u e q", u=2, e=2),
            in0=pair_sums[:, 0, :].rearrange("b (u q e) -> b u e q", u=2, e=2),
            in1=pair_sums[:, 1, :].rearrange("b (u q e) -> b u e q", u=2, e=2),
            op=ALU.add,
        )

        key_grouped = transpose_words(nc, banks, pool, key_sb, identity, nc.scalar.copy, "key")
        sum_T = sums.tile([P, PACK, P], F32)
        for t in range(PACK):
            nc.tensor.transpose(sum_T[:, t, :], position_sum[:, P * t : P * (t + 1)], identity[:])
        mean_grouped = pool.tile([P, P * PACK], BF16, align_bytes=64)
        nc.scalar.mul(
            out=mean_grouped[:].rearrange("p (b t) -> p b t", t=PACK),
            in_=sum_T[:].rearrange("p t b -> p b t"),
            mul=1.0 / POSITIONS,
        )
        key_codes, key_scales = quantise(nc, pool, key_grouped, D, "key")
        mean_codes, mean_scales = quantise(nc, pool, mean_grouped, P, "mean")

        erase_grouped = transpose_words(nc, banks, pool, erase_sb, identity, nc.scalar.copy, "erase")

        proj_T = sums.tile([P, PACK, P], F32)
        for t in range(PACK):
            rows = slice(P * t, P * (t + 1))
            one_pass(nc, proj_T[:, t, :], (key_codes[:, rows], key_scales[:, rows]), (mean_codes[:], mean_scales[:]))
        proj_grouped = pool.tile([P, P * PACK], BF16, align_bytes=64)
        nc.scalar.copy(
            out=proj_grouped[:].rearrange("p (b t) -> p b t", t=PACK),
            in_=proj_T[:].rearrange("p t b -> p b t"),
        )
        erase_codes, erase_scales = quantise(nc, pool, erase_grouped, D, "erase")
        proj_codes, proj_scales = quantise(nc, pool, proj_grouped, P, "proj")

        add_grouped = transpose_words(nc, banks, pool, add_sb, identity, nc.scalar.copy, "add")

        erase_ps = sums.tile([P, D], F32)
        one_pass(nc, erase_ps[:], (proj_codes[:], proj_scales[:]), (erase_codes[:], erase_scales[:]))
        keep = pool.tile([P, D], F32)
        nc.scalar.activation(out=keep[:], in_=erase_ps[:], func=ACT.Sigmoid, scale=-1.0)
        nc.scalar.activation(out=warm_col[:, 1:2], in_=keep[:, 0:1], func=ACT.Abs_reciprocal_sqrt)
        add_codes, add_scales = quantise(nc, pool, add_grouped, D, "add")
        add_ps = sums.tile([P, D], F32)
        one_pass(nc, add_ps[:], (proj_codes[:], proj_scales[:]), (add_codes[:], add_scales[:]))

        gated = pool.tile([P, SLOTS, D], F32)
        x = pool.tile([P, SLOTS, D], F32)
        squares = pool.tile([P, SLOTS, D], F32)
        normed = pool.tile([P, SLOTS, D], F32)
        x_sum = pool.tile([P, SLOTS], F32)
        neg_mean = pool.tile([P, SLOTS], F32)
        sq_sum = pool.tile([P, SLOTS], F32)
        rstd = pool.tile([P, SLOTS], F32)
        shift = pool.tile([P, SLOTS], F32)

        def gate_on_vector(m):
            cols = slice(0, D if m == 0 else VECTOR_COLUMNS)
            nc.vector.tensor_tensor(out=gated[:, m, cols], in0=memory_sb[:, m, cols], in1=keep[:, cols], op=ALU.mult)

        def gate_on_gpsimd(m):
            cols = slice(VECTOR_COLUMNS, D)
            nc.gpsimd.tensor_tensor(out=gated[:, m, cols], in0=memory_sb[:, m, cols], in1=keep[:, cols], op=ALU.mult)

        def add_and_sum(m):
            nc.vector.scalar_tensor_tensor(
                out=x[:, m, :],
                in0=gated[:, m, :],
                scalar=1.0,
                in1=add_ps[:],
                op0=ALU.mult,
                op1=ALU.add,
                accum_out=x_sum[:, m : m + 1],
            )
            if m >= SLOTS - VECTOR_NORM_SLOTS:
                nc.gpsimd.tensor_scalar_mul(out=neg_mean[:, m : m + 1], in0=x_sum[:, m : m + 1], scalar1=-1.0 / D)

        def square_and_sum(m):
            nc.scalar.activation(
                out=squares[:, m, :],
                in_=x[:, m, :],
                func=ACT.Square,
                scale=-1.0 * D,
                bias=x_sum[:, m : m + 1],
                accum_out=sq_sum[:, m : m + 1],
            )

        def scale_and_shift(m):
            nc.scalar.activation(
                out=rstd[:, m : m + 1],
                in_=sq_sum[:, m : m + 1],
                func=ACT.Abs_reciprocal_sqrt,
                scale=1.0 / (D * D * D),
                bias=eps_col[:],
            )
            if m < SLOTS - VECTOR_NORM_SLOTS:
                nc.gpsimd.tensor_scalar(
                    out=shift[:, m : m + 1],
                    in0=x_sum[:, m : m + 1],
                    scalar1=rstd[:, m : m + 1],
                    scalar2=-1.0 / D,
                    op0=ALU.mult,
                    op1=ALU.mult,
                )

        def normalise_and_store(m):
            col = slice(m, m + 1)
            if m < SLOTS - VECTOR_NORM_SLOTS:
                nc.scalar.activation(
                    out=normed[:, m, :], in_=x[:, m, :], func=ACT.Identity, scale=rstd[:, col], bias=shift[:, col]
                )
            else:
                nc.vector.tensor_scalar(
                    out=normed[:, m, :],
                    in0=x[:, m, :],
                    scalar1=neg_mean[:, col],
                    scalar2=rstd[:, col],
                    op0=ALU.add,
                    op1=ALU.mult,
                )
            nc.sync.dma_start(out=out[:, m, :], in_=normed[:, m, :])

        gate_on_vector(0)
        gate_on_gpsimd(1)
        for m in range(SLOTS + LAG):
            if m + 1 < SLOTS:
                gate_on_vector(m + 1)
            if m + 2 < SLOTS:
                gate_on_gpsimd(m + 2)
            if m < SLOTS:
                add_and_sum(m)
                square_and_sum(m)
            if m >= LAG:
                normalise_and_store(m - LAG)
            if m < SLOTS:
                scale_and_shift(m)
